import numpy as np
import ml_dtypes


def mxq(x, axis, fmt="e4m3"):
    dtype, down = {"e4m3": (ml_dtypes.float8_e4m3fn, 7), "e5m2": (ml_dtypes.float8_e5m2, 14)}[fmt]
    v = np.moveaxis(np.asarray(x, np.float32).astype(ml_dtypes.bfloat16).astype(np.float64), axis, -1)
    blocks = v.reshape(v.shape[:-1] + (-1, 32))
    amax = np.abs(blocks).max(-1, keepdims=True)
    byte = np.maximum(np.where(amax > 0, np.frexp(amax)[1] - 1 + 127, 0) - down, 1)
    scale = np.exp2(byte - 127.0)
    codes = (blocks / scale).astype(np.float32).astype(dtype).astype(np.float64)
    return np.moveaxis((codes * scale).reshape(v.shape), -1, axis)


WIDE = False


def mx_kscale(k):
    if not WIDE:
        return np.ones(k)
    levels = np.array([10, -10, 5, -5, 0])
    a = np.random.permutation(np.resize(levels, k // 512 * 4)).reshape(k // 512, 4)
    idx = np.arange(k)
    return np.exp2(a[idx // 512, idx % 128 // 32])


BF16 = ml_dtypes.bfloat16


def bf(x):
    return np.asarray(x, np.float32).astype(BF16)


def f64(x):
    return np.asarray(x).astype(np.float64)


B, D, H = 4096, 512, 512
C = D + H
EPS = 1e-3


def sigmoid(v):
    return 1.0 / (1.0 + np.exp(-v))


def layer_norm(v, gamma, beta):
    m = v.mean(-1, keepdims=True)
    var = v.var(-1, keepdims=True)
    return (v - m) / np.sqrt(var + EPS) * gamma + beta


def setup_inputs():
    s = mx_kscale(D)
    t = mx_kscale(H)
    w_u = np.random.standard_normal((C, H)) / np.sqrt(C)
    w_u[:D] = w_u[:D] / s[:, None]
    g = np.random.standard_normal((B, H))
    return {"x": bf(np.random.standard_normal((B, D)) * s),
            "hidden_state": bf(np.random.standard_normal((B, H))),
            "swiglu": bf(g / (1.0 + np.exp(-g)) * np.random.standard_normal((B, H))),
            "W_u": bf(w_u),
            "b_u": bf(np.random.standard_normal(H) * 0.3),
            "gamma_h": bf((1.0 + 0.1 * np.random.standard_normal(H)) * t),
            "beta_h": bf(0.1 * np.random.standard_normal(H) * t),
            "W_d": bf(np.random.standard_normal((H, D)) / np.sqrt(H) / t[:, None]),
            "b_d": bf(np.random.standard_normal(D) * 0.3),
            "gamma_o": bf(1.0 + 0.1 * np.random.standard_normal(D)),
            "beta_o": bf(0.1 * np.random.standard_normal(D))}


def reference(x, hidden_state, swiglu, W_u, b_u, gamma_h, beta_h, W_d, b_d, gamma_o, beta_o):
    h = f64(hidden_state)
    combined = np.concatenate([f64(x), h], axis=-1)
    u = sigmoid((mxq(combined, 1, "e4m3") @ mxq(f64(W_u), 0, "e4m3")) + f64(b_u))
    new_h = layer_norm((1.0 - u) * h + u * f64(swiglu) + h, f64(gamma_h), f64(beta_h))
    out = layer_norm((mxq(new_h, 1, "e4m3") @ mxq(f64(W_d), 0, "e4m3")) + f64(b_d), f64(gamma_o), f64(beta_o))
    return out, new_h

@@ -1,0 +1,357 @@
+from contextlib import ExitStack
+
+import concourse.mybir as mybir
+from concourse.masks import make_identity
+
+F32 = mybir.dt.float32
+BF16 = mybir.dt.bfloat16
+U32 = mybir.dt.uint32
+U8 = mybir.dt.uint8
+FP8X4 = mybir.dt.float8_e4m3fn_x4
+ALU = mybir.AluOpType
+ACT = mybir.ActivationFunctionType
+
+P = 128
+PACK = 4
+B, D, H = 4096, 512, 512
+EPS = 1e-3
+CHUNKS = H // P
+SUB = 2
+TOK = SUB * P
+GROUPS = B // TOK
+BANK = 512
+CPB = BANK // TOK
+LOOKAHEAD = 3
+
+FLOPS = 2 * B * (D + H) * H + 2 * B * H * D
+
+
+def quantise_weight(nc, prep, keep, raw, passes, width, label):
+    quads = prep.tile([P, passes, width, PACK], BF16, align_bytes=64, name=label + "_quads")
+    for c in range(passes):
+        nc.vector.tensor_copy(out=quads[:, c], in_=raw[:, c].rearrange("p t n -> p n t"))
+    codes = keep.tile([P, passes, width], U32, align_bytes=64, name=label + "_codes")
+    scales = keep.tile([P, passes, width], U8, align_bytes=64, name=label + "_scales")
+    nc.vector.quantize_mx(
+        out=codes[:].rearrange("p c n -> p (c n)").bitcast(FP8X4),
+        scales=scales[:].rearrange("p c n -> p (c n)"),
+        in_=quads[:].rearrange("p c n t -> p (c n t)"),
+    )
+    return codes, scales
+
+
+def tile_recurrentffn_pb_t_kernel(
+    tc, x, hidden_state, swiglu, W_u, b_u, gamma_h, beta_h, W_d, b_d, gamma_o, beta_o, out_0, out_1
+):
+    nc = tc.nc
+    x_v = x.rearrange("(p j) d -> p j d", p=P)
+    h_v = hidden_state.rearrange("(p j) d -> p j d", p=P)
+    s_v = swiglu.rearrange("(p j) d -> p j d", p=P)
+    out_v = out_0.rearrange("(p j) d -> p j d", p=P)
+    newh_v = out_1.rearrange("(p j) d -> p j d", p=P)
+
+    with ExitStack() as ctx:
+        ctx.enter_context(tc.manual_schedule())
+        keep = ctx.enter_context(tc.tile_pool(name="keep", bufs=1))
+        prep = ctx.enter_context(tc.tile_pool(name="prep", bufs=1))
+        inp = ctx.enter_context(tc.tile_pool(name="inp", bufs=5))
+        work = ctx.enter_context(tc.tile_pool(name="work", bufs=2))
+        rows = ctx.enter_context(tc.tile_pool(name="rows", bufs=3))
+        stat = ctx.enter_context(tc.tile_pool(name="stat", bufs=8))
+        psum = ctx.enter_context(tc.psum_pool(name="psum", bufs=8))
+
+        live = {}
+
+        def group_rows(g):
+            return slice(g * SUB, (g + 1) * SUB)
+
+        def load_inputs(g):
+            x_sb = inp.tile([P, SUB, D], BF16)
+            nc.sync.dma_start(out=x_sb[:], in_=x_v[:, group_rows(g), :])
+            h_sb = inp.tile([P, SUB, H], BF16)
+            nc.sync.dma_start(out=h_sb[:], in_=h_v[:, group_rows(g), :])
+            s_sb = inp.tile([P, SUB, H], BF16)
+            nc.sync.dma_start(out=s_sb[:], in_=s_v[:, group_rows(g), :])
+            live["x", g], live["h", g], live["s", g] = x_sb, h_sb, s_sb
+
+        ident = keep.tile([P, P], F32)
+        make_identity(nc, ident[:])
+        neg_half = keep.tile([P, 1], F32)
+        nc.gpsimd.memset(neg_half[:], -0.5)
+
+        load_inputs(0)
+        wu_raw = prep.tile([P, 2, PACK, H], BF16)
+        nc.sync.dma_start(
+            out=wu_raw[:].rearrange("p c (u e) n -> p (c u) (e n)", e=2),
+            in_=W_u.rearrange("(cu p e) n -> p cu (e n)", p=P, e=2),
+        )
+        wd_raw = prep.tile([P, 1, PACK, D], BF16)
+        nc.sync.dma_start(out=wd_raw[:, 0], in_=W_d.rearrange("(m p) n -> p m n", p=P))
+        for g in range(1, LOOKAHEAD - 1):
+            load_inputs(g)
+
+        vec_rows = prep.tile([P, P], BF16)
+        nc.vector.memset(vec_rows[:], 0.0)
+        for v, vec in enumerate((b_u, gamma_h, beta_h)):
+            nc.scalar.dma_start(
+                out=vec_rows[v * CHUNKS : (v + 1) * CHUNKS, :], in_=vec.rearrange("(m j) -> m j", j=P)
+            )
+        vec_rows_f32 = prep.tile([P, P], F32)
+        nc.vector.tensor_copy(out=vec_rows_f32[:], in_=vec_rows[:])
+        vec_cols_ps = psum.tile([P, P], F32, tag="bank")
+        nc.tensor.transpose(vec_cols_ps[:], vec_rows_f32[:], ident[:])
+        vec_cols = keep.tile([P, 3 * CHUNKS], F32)
+        nc.vector.tensor_copy(out=vec_cols[:], in_=vec_cols_ps[:, : 3 * CHUNKS])
+
+        def column(v, m):
+            return vec_cols[:, v * CHUNKS + m : v * CHUNKS + m + 1]
+
+        bd_all = keep.tile([P, D], BF16)
+        nc.scalar.dma_start(out=bd_all[:], in_=b_d.partition_broadcast(P))
+        go_all = keep.tile([P, D], BF16)
+        nc.scalar.dma_start(out=go_all[:], in_=gamma_o.partition_broadcast(P))
+        bo_all = keep.tile([P, D], BF16)
+        nc.scalar.dma_start(out=bo_all[:], in_=beta_o.partition_broadcast(P))
+
+        wu_codes, wu_scales = quantise_weight(nc, prep, keep, wu_raw, 2, H, "wu")
+        wd_codes, wd_scales = quantise_weight(nc, prep, keep, wd_raw, 1, D, "wd")
+
+        def negative_mean(sum_v, width):
+            neg_mean = stat.tile([P, 1], F32)
+            nc.gpsimd.tensor_scalar(
+                out=neg_mean[:], in0=sum_v[:], scalar1=-1.0 / width, scalar2=0.0, op0=ALU.mult, op1=ALU.add
+            )
+            return neg_mean
+
+        def inverse_deviation(v, neg_mean, width):
+            squares = rows.tile([P, width], BF16)
+            sum_sq = stat.tile([P, 1], F32)
+            nc.scalar.activation(
+                out=squares[:], in_=v[:], func=ACT.Square, bias=neg_mean[:], scale=1.0, accum_out=sum_sq[:]
+            )
+            var_eps = stat.tile([P, 1], F32)
+            nc.gpsimd.tensor_scalar(
+                out=var_eps[:], in0=sum_sq[:], scalar1=1.0 / width, scalar2=EPS, op0=ALU.mult, op1=ALU.add
+            )
+            rstd = stat.tile([P, 1], F32)
+            nc.gpsimd.tensor_tensor(out=rstd[:], in0=var_eps[:], in1=neg_half[:], op=ALU.pow)
+            return rstd
+
+        def turn_inputs(g):
+            for t in range(SUB):
+                xhT = psum.tile([P, 2, 2, P], F32, tag="bank")
+                for c, src in enumerate((live["x", g], live["h", g])):
+                    src_words = src[:, t, :].bitcast(F32)
+                    for u in range(2):
+                        nc.tensor.transpose(xhT[:, c, u, :], src_words[:, u * P : (u + 1) * P], ident[:])
+                live["xhT", g, t] = xhT
+
+        def copy_inputs_out(g):
+            xh_quads = work.tile([P, 2 * TOK * PACK], BF16, align_bytes=64)
+            xh_words = xh_quads[:].bitcast(F32).rearrange("q (c k u) -> q c k u", c=2, u=2)
+            for t in range(SUB):
+                nc.scalar.copy(
+                    out=xh_words[:, :, t * P : (t + 1) * P, :],
+                    in_=live["xhT", g, t][:].rearrange("q c u k -> q c k u"),
+                )
+            live["xh_quads", g] = xh_quads
+
+        def quantise_inputs(g):
+            xh_codes = work.tile([P, 2, TOK], U32, align_bytes=64)
+            xh_scales = work.tile([P, 2, TOK], U8, align_bytes=64)
+            nc.vector.quantize_mx(
+                out=xh_codes[:].rearrange("q c k -> q (c k)").bitcast(FP8X4),
+                scales=xh_scales[:].rearrange("q c k -> q (c k)"),
+                in_=live["xh_quads", g][:],
+            )
+            live["xh_codes", g], live["xh_scales", g] = xh_codes, xh_scales
+
+        def gate_matmul(g):
+            for b in range(CHUNKS // CPB):
+                zT = psum.tile([P, CPB, TOK], F32, tag="bank")
+                for i in range(CPB):
+                    m = b * CPB + i
+                    for c in range(2):
+                        nc.tensor.matmul_mx(
+                            out=zT[:, i, :],
+                            lhsT=wu_codes[:, c, m * P : (m + 1) * P].bitcast(FP8X4),
+                            lhsT_scale=wu_scales[:, c, m * P : (m + 1) * P],
+                            rhs=live["xh_codes", g][:, c, :].bitcast(FP8X4),
+                            rhs_scale=live["xh_scales", g][:, c, :],
+                            start=(c == 0),
+                            stop=(c == 1),
+                        )
+                live["zT", g, b] = zT
+
+        def gate_sigmoid(g):
+            uT = work.tile([P, CHUNKS, TOK], F32)
+            for b in range(CHUNKS // CPB):
+                for i in range(CPB):
+                    m = b * CPB + i
+                    nc.scalar.activation(
+                        out=uT[:, m, :], in_=live["zT", g, b][:, i, :], func=ACT.Sigmoid,
+                        bias=column(0, m), scale=1.0,
+                    )
+            live["uT", g] = uT
+
+        def turn_gate_back(g):
+            for t in range(SUB):
+                u_ps = psum.tile([P, H], F32, tag="bank")
+                for m in range(CHUNKS):
+                    nc.tensor.transpose(
+                        u_ps[:, m * P : (m + 1) * P], live["uT", g][:, m, t * P : (t + 1) * P], ident[:]
+                    )
+                live["u", g, t] = u_ps
+
+        def difference(g):
+            diff = work.tile([P, SUB, H], F32, bufs=3)
+            nc.vector.tensor_tensor(out=diff[:], in0=live["s", g][:], in1=live["h", g][:], op=ALU.subtract)
+            live["diff", g] = diff
+
+        def blend(g):
+            for t in range(SUB):
+                gated = rows.tile([P, H], F32)
+                nc.vector.tensor_tensor(
+                    out=gated[:], in0=live["u", g, t][:], in1=live["diff", g][:, t, :], op=ALU.mult
+                )
+                blended = rows.tile([P, H], F32, bufs=2 * SUB)
+                sum_p = stat.tile([P, 1], F32)
+                nc.vector.scalar_tensor_tensor(
+                    out=blended[:], in0=live["h", g][:, t, :], scalar=2.0, in1=gated[:],
+                    op0=ALU.mult, op1=ALU.add, accum_out=sum_p[:],
+                )
+                live["p", g, t] = blended
+                live["p_neg_mean", g, t] = negative_mean(sum_p, H)
+
+        def first_variance(g):
+            for t in range(SUB):
+                neg_mean = live["p_neg_mean", g, t]
+                rstd = inverse_deviation(live["p", g, t], neg_mean, H)
+                shift = stat.tile([P, 1], F32)
+                nc.gpsimd.tensor_tensor(out=shift[:], in0=neg_mean[:], in1=rstd[:], op=ALU.mult)
+                live["p_rstd", g, t], live["p_shift", g, t] = rstd, shift
+
+        def normalise(g):
+            normed = work.tile([P, SUB, H], F32)
+            for t in range(SUB):
+                nc.scalar.activation(
+                    out=normed[:, t, :], in_=live["p", g, t][:], func=ACT.Identity,
+                    scale=live["p_rstd", g, t][:], bias=live["p_shift", g, t][:],
+                )
+            live["normed", g] = normed
+
+        def turn_normed(g):
+            for b in range(CHUNKS // CPB):
+                nT = psum.tile([P, CPB, TOK], F32, tag="bank")
+                for i in range(CPB):
+                    m = b * CPB + i
+                    for t in range(SUB):
+                        nc.tensor.transpose(
+                            nT[:, i, t * P : (t + 1) * P], live["normed", g][:, t, m * P : (m + 1) * P], ident[:]
+                        )
+                live["nT", g, b] = nT
+
+        def apply_gain(g):
+            nhT = work.tile([P, CHUNKS, TOK], F32)
+            for b in range(CHUNKS // CPB):
+                for i in range(CPB):
+                    m = b * CPB + i
+                    nc.scalar.activation(
+                        out=nhT[:, m, :], in_=live["nT", g, b][:, i, :], func=ACT.Identity,
+                        scale=column(1, m), bias=column(2, m),
+                    )
+            live["nhT", g] = nhT
+
+        def quantise_state(g):
+            nh_quads = work.tile([P, TOK, PACK], BF16, align_bytes=64)
+            nc.vector.tensor_copy(out=nh_quads[:], in_=live["nhT", g][:].rearrange("j m k -> j k m"))
+            nh_codes = work.tile([P, TOK], U32, align_bytes=64)
+            nh_scales = work.tile([P, TOK], U8, align_bytes=64)
+            nc.vector.quantize_mx(
+                out=nh_codes[:].bitcast(FP8X4), scales=nh_scales[:], in_=nh_quads[:].rearrange("j k m -> j (k m)")
+            )
+            live["nh_codes", g], live["nh_scales", g] = nh_codes, nh_scales
+
+        def turn_state_back(g):
+            for t in range(SUB):
+                nh_ps = psum.tile([P, H], F32, tag="bank")
+                for m in range(CHUNKS):
+                    nc.tensor.transpose(
+                        nh_ps[:, m * P : (m + 1) * P], live["nhT", g][:, m, t * P : (t + 1) * P], ident[:]
+                    )
+                live["nh", g, t] = nh_ps
+
+        def store_state(g):
+            nh_rows = work.tile([P, SUB, H], F32, bufs=3)
+            for t in range(SUB):
+                nc.scalar.copy(out=nh_rows[:, t, :], in_=live["nh", g, t][:])
+            nc.sync.dma_start(out=newh_v[:, group_rows(g), :], in_=nh_rows[:])
+
+        def output_matmul(g):
+            for t in range(SUB):
+                y_ps = psum.tile([P, D], F32, tag="bank")
+                nc.tensor.matmul_mx(
+                    out=y_ps[:],
+                    lhsT=live["nh_codes", g][:, t * P : (t + 1) * P].bitcast(FP8X4),
+                    lhsT_scale=live["nh_scales", g][:, t * P : (t + 1) * P],
+                    rhs=wd_codes[:, 0, :].bitcast(FP8X4),
+                    rhs_scale=wd_scales[:, 0, :],
+                    start=True,
+                    stop=True,
+                )
+                live["y", g, t] = y_ps
+
+        def add_bias(g):
+            for t in range(SUB):
+                biased = rows.tile([P, D], F32, bufs=2 * SUB + 1)
+                sum_y = stat.tile([P, 1], F32)
+                nc.vector.scalar_tensor_tensor(
+                    out=biased[:], in0=live["y", g, t][:], scalar=1.0, in1=bd_all[:],
+                    op0=ALU.mult, op1=ALU.add, accum_out=sum_y[:],
+                )
+                live["yb", g, t] = biased
+                live["y_neg_mean", g, t] = negative_mean(sum_y, D)
+
+        def second_variance(g):
+            for t in range(SUB):
+                live["y_rstd", g, t] = inverse_deviation(live["yb", g, t], live["y_neg_mean", g, t], D)
+
+        def finish_output(g):
+            out_rows = work.tile([P, SUB, D], F32, bufs=3)
+            for t in range(SUB):
+                gained = rows.tile([P, D], F32)
+                nc.vector.scalar_tensor_tensor(
+                    out=gained[:], in0=live["yb", g, t][:], scalar=live["y_neg_mean", g, t][:], in1=go_all[:],
+                    op0=ALU.add, op1=ALU.mult,
+                )
+                nc.vector.scalar_tensor_tensor(
+                    out=out_rows[:, t, :], in0=gained[:], scalar=live["y_rstd", g, t][:], in1=bo_all[:],
+                    op0=ALU.mult, op1=ALU.add,
+                )
+            nc.sync.dma_start(out=out_v[:, group_rows(g), :], in_=out_rows[:])
+
+        def on(stage, g):
+            if 0 <= g < GROUPS:
+                stage(g)
+
+        for s in range(-1, GROUPS + 3):
+            on(load_inputs, s + LOOKAHEAD)
+            on(copy_inputs_out, s)
+            on(blend, s - 1)
+            on(turn_normed, s - 2)
+            on(apply_gain, s - 2)
+            on(quantise_inputs, s)
+            on(turn_state_back, s - 2)
+            on(quantise_state, s - 2)
+            on(second_variance, s - 3)
+            on(gate_matmul, s)
+            on(difference, s + 1)
+            on(first_variance, s - 1)
+            on(output_matmul, s - 2)
+            on(store_state, s - 2)
+            on(finish_output, s - 3)
+            on(turn_inputs, s + 1)
+            on(gate_sigmoid, s)
+            on(add_bias, s - 2)
+            on(turn_gate_back, s)
+            on(normalise, s - 1)

@@ -26,8 +26,8 @@ LOOKAHEAD = 3
 FLOPS = 2 * B * (D + H) * H + 2 * B * H * D
 
 
-def quantise_weight(nc, prep, keep, raw, passes, width, label):
-    quads = prep.tile([P, passes, width, PACK], BF16, align_bytes=64, name=label + "_quads")
+def quantise_weight(nc, pool, keep, raw, passes, width, label):
+    quads = pool.tile([P, passes, width, PACK], BF16, align_bytes=64, name=label + "_quads", bufs=1)
     for c in range(passes):
         nc.vector.tensor_copy(out=quads[:, c], in_=raw[:, c].rearrange("p t n -> p n t"))
     codes = keep.tile([P, passes, width], U32, align_bytes=64, name=label + "_codes")
@@ -53,10 +53,9 @@ def tile_recurrentffn_pb_t_kernel(
     with ExitStack() as ctx:
         ctx.enter_context(tc.manual_schedule())
         keep = ctx.enter_context(tc.tile_pool(name="keep", bufs=1))
-        prep = ctx.enter_context(tc.tile_pool(name="prep", bufs=1))
-        inp = ctx.enter_context(tc.tile_pool(name="inp", bufs=5))
-        work = ctx.enter_context(tc.tile_pool(name="work", bufs=2))
-        rows = ctx.enter_context(tc.tile_pool(name="rows", bufs=3))
+        hold = ctx.enter_context(tc.tile_pool(name="hold", bufs=GROUPS))
+        inp = ctx.enter_context(tc.tile_pool(name="inp", bufs=4))
+        early = ctx.enter_context(tc.tile_pool(name="early", bufs=2))
         stat = ctx.enter_context(tc.tile_pool(name="stat", bufs=8))
         psum = ctx.enter_context(tc.psum_pool(name="psum", bufs=8))
 
@@ -68,7 +67,7 @@ def tile_recurrentffn_pb_t_kernel(
         def load_inputs(g):
             x_sb = inp.tile([P, SUB, D], BF16)
             nc.sync.dma_start(out=x_sb[:], in_=x_v[:, group_rows(g), :])
-            h_sb = inp.tile([P, SUB, H], BF16)
+            h_sb = inp.tile([P, SUB, H], BF16, bufs=6)
             nc.sync.dma_start(out=h_sb[:], in_=h_v[:, group_rows(g), :])
             s_sb = inp.tile([P, SUB, H], BF16)
             nc.sync.dma_start(out=s_sb[:], in_=s_v[:, group_rows(g), :])
@@ -76,66 +75,45 @@ def tile_recurrentffn_pb_t_kernel(
 
         ident = keep.tile([P, P], F32)
         make_identity(nc, ident[:])
-        neg_half = keep.tile([P, 1], F32)
-        nc.gpsimd.memset(neg_half[:], -0.5)
+        eps_col = keep.tile([P, 1], F32)
+        nc.gpsimd.memset(eps_col[:], EPS)
 
-        load_inputs(0)
-        wu_raw = prep.tile([P, 2, PACK, H], BF16)
-        nc.sync.dma_start(
-            out=wu_raw[:].rearrange("p c (u e) n -> p (c u) (e n)", e=2),
-            in_=W_u.rearrange("(cu p e) n -> p cu (e n)", p=P, e=2),
-        )
-        wd_raw = prep.tile([P, 1, PACK, D], BF16)
-        nc.sync.dma_start(out=wd_raw[:, 0], in_=W_d.rearrange("(m p) n -> p m n", p=P))
-        for g in range(1, LOOKAHEAD - 1):
-            load_inputs(g)
-
-        vec_rows = prep.tile([P, P], BF16)
-        nc.vector.memset(vec_rows[:], 0.0)
-        for v, vec in enumerate((b_u, gamma_h, beta_h)):
-            nc.scalar.dma_start(
-                out=vec_rows[v * CHUNKS : (v + 1) * CHUNKS, :], in_=vec.rearrange("(m j) -> m j", j=P)
+        with tc.tile_pool(name="prep", bufs=1) as prep:
+            wu_raw = prep.tile([P, 2, PACK, H], BF16)
+            nc.sync.dma_start(
+                out=wu_raw[:].rearrange("p c (u e) n -> p (c u) (e n)", e=2),
+                in_=W_u.rearrange("(cu p e) n -> p cu (e n)", p=P, e=2),
             )
-        vec_rows_f32 = prep.tile([P, P], F32)
-        nc.vector.tensor_copy(out=vec_rows_f32[:], in_=vec_rows[:])
-        vec_cols_ps = psum.tile([P, P], F32, tag="bank")
-        nc.tensor.transpose(vec_cols_ps[:], vec_rows_f32[:], ident[:])
-        vec_cols = keep.tile([P, 3 * CHUNKS], F32)
-        nc.vector.tensor_copy(out=vec_cols[:], in_=vec_cols_ps[:, : 3 * CHUNKS])
+            for g in range(LOOKAHEAD - 1):
+                load_inputs(g)
+
+            vec_rows = prep.tile([P, P], BF16)
+            nc.vector.memset(vec_rows[:], 0.0)
+            for v, vec in enumerate((b_u, gamma_h, beta_h)):
+                nc.scalar.dma_start(
+                    out=vec_rows[v * CHUNKS : (v + 1) * CHUNKS, :], in_=vec.rearrange("(m j) -> m j", j=P)
+                )
+            vec_rows_f32 = prep.tile([P, P], F32)
+            nc.vector.tensor_copy(out=vec_rows_f32[:], in_=vec_rows[:])
+            vec_cols_ps = psum.tile([P, P], F32, tag="bank")
+            nc.tensor.transpose(vec_cols_ps[:], vec_rows_f32[:], ident[:])
+            vec_cols = keep.tile([P, 3 * CHUNKS], F32)
+            nc.vector.tensor_copy(out=vec_cols[:], in_=vec_cols_ps[:, : 3 * CHUNKS])
+            wu_codes, wu_scales = quantise_weight(nc, prep, keep, wu_raw, 2, H, "wu")
 
         def column(v, m):
             return vec_cols[:, v * CHUNKS + m : v * CHUNKS + m + 1]
 
+        late = ctx.enter_context(tc.tile_pool(name="late", bufs=2))
+
+        wd_raw = late.tile([P, 1, PACK, D], BF16, bufs=1)
+        nc.gpsimd.dma_start(out=wd_raw[:, 0], in_=W_d.rearrange("(m p) n -> p m n", p=P))
         bd_all = keep.tile([P, D], BF16)
-        nc.scalar.dma_start(out=bd_all[:], in_=b_d.partition_broadcast(P))
+        nc.gpsimd.dma_start(out=bd_all[:], in_=b_d.partition_broadcast(P))
         go_all = keep.tile([P, D], BF16)
-        nc.scalar.dma_start(out=go_all[:], in_=gamma_o.partition_broadcast(P))
+        nc.gpsimd.dma_start(out=go_all[:], in_=gamma_o.partition_broadcast(P))
         bo_all = keep.tile([P, D], BF16)
-        nc.scalar.dma_start(out=bo_all[:], in_=beta_o.partition_broadcast(P))
-
-        wu_codes, wu_scales = quantise_weight(nc, prep, keep, wu_raw, 2, H, "wu")
-        wd_codes, wd_scales = quantise_weight(nc, prep, keep, wd_raw, 1, D, "wd")
-
-        def negative_mean(sum_v, width):
-            neg_mean = stat.tile([P, 1], F32)
-            nc.gpsimd.tensor_scalar(
-                out=neg_mean[:], in0=sum_v[:], scalar1=-1.0 / width, scalar2=0.0, op0=ALU.mult, op1=ALU.add
-            )
-            return neg_mean
-
-        def inverse_deviation(v, neg_mean, width):
-            squares = rows.tile([P, width], BF16)
-            sum_sq = stat.tile([P, 1], F32)
-            nc.scalar.activation(
-                out=squares[:], in_=v[:], func=ACT.Square, bias=neg_mean[:], scale=1.0, accum_out=sum_sq[:]
-            )
-            var_eps = stat.tile([P, 1], F32)
-            nc.gpsimd.tensor_scalar(
-                out=var_eps[:], in0=sum_sq[:], scalar1=1.0 / width, scalar2=EPS, op0=ALU.mult, op1=ALU.add
-            )
-            rstd = stat.tile([P, 1], F32)
-            nc.gpsimd.tensor_tensor(out=rstd[:], in0=var_eps[:], in1=neg_half[:], op=ALU.pow)
-            return rstd
+        nc.gpsimd.dma_start(out=bo_all[:], in_=beta_o.partition_broadcast(P))
 
         def turn_inputs(g):
             for t in range(SUB):
@@ -147,7 +125,7 @@ def tile_recurrentffn_pb_t_kernel(
                 live["xhT", g, t] = xhT
 
         def copy_inputs_out(g):
-            xh_quads = work.tile([P, 2 * TOK * PACK], BF16, align_bytes=64)
+            xh_quads = early.tile([P, 2 * TOK * PACK], BF16, align_bytes=64)
             xh_words = xh_quads[:].bitcast(F32).rearrange("q (c k u) -> q c k u", c=2, u=2)
             for t in range(SUB):
                 nc.scalar.copy(
@@ -157,8 +135,8 @@ def tile_recurrentffn_pb_t_kernel(
             live["xh_quads", g] = xh_quads
 
         def quantise_inputs(g):
-            xh_codes = work.tile([P, 2, TOK], U32, align_bytes=64)
-            xh_scales = work.tile([P, 2, TOK], U8, align_bytes=64)
+            xh_codes = early.tile([P, 2, TOK], U32, align_bytes=64)
+            xh_scales = early.tile([P, 2, TOK], U8, align_bytes=64)
             nc.vector.quantize_mx(
                 out=xh_codes[:].rearrange("q c k -> q (c k)").bitcast(FP8X4),
                 scales=xh_scales[:].rearrange("q c k -> q (c k)"),
@@ -184,7 +162,7 @@ def tile_recurrentffn_pb_t_kernel(
                 live["zT", g, b] = zT
 
         def gate_sigmoid(g):
-            uT = work.tile([P, CHUNKS, TOK], F32)
+            uT = early.tile([P, CHUNKS, TOK], F32)
             for b in range(CHUNKS // CPB):
                 for i in range(CPB):
                     m = b * CPB + i
@@ -204,39 +182,64 @@ def tile_recurrentffn_pb_t_kernel(
                 live["u", g, t] = u_ps
 
         def difference(g):
-            diff = work.tile([P, SUB, H], F32, bufs=3)
+            diff = early.tile([P, SUB, H], F32, bufs=4)
             nc.vector.tensor_tensor(out=diff[:], in0=live["s", g][:], in1=live["h", g][:], op=ALU.subtract)
             live["diff", g] = diff
 
         def blend(g):
+            gated = early.tile([P, SUB, H], F32)
+            blended = hold.tile([P, SUB, H], F32)
+            sum_p = hold.tile([P, SUB], F32)
             for t in range(SUB):
-                gated = rows.tile([P, H], F32)
                 nc.vector.tensor_tensor(
-                    out=gated[:], in0=live["u", g, t][:], in1=live["diff", g][:, t, :], op=ALU.mult
+                    out=gated[:, t, :], in0=live["u", g, t][:], in1=live["diff", g][:, t, :], op=ALU.mult
                 )
-                blended = rows.tile([P, H], F32, bufs=2 * SUB)
-                sum_p = stat.tile([P, 1], F32)
-                nc.vector.scalar_tensor_tensor(
-                    out=blended[:], in0=live["h", g][:, t, :], scalar=2.0, in1=gated[:],
-                    op0=ALU.mult, op1=ALU.add, accum_out=sum_p[:],
-                )
-                live["p", g, t] = blended
-                live["p_neg_mean", g, t] = negative_mean(sum_p, H)
-
-        def first_variance(g):
             for t in range(SUB):
-                neg_mean = live["p_neg_mean", g, t]
-                rstd = inverse_deviation(live["p", g, t], neg_mean, H)
-                shift = stat.tile([P, 1], F32)
-                nc.gpsimd.tensor_tensor(out=shift[:], in0=neg_mean[:], in1=rstd[:], op=ALU.mult)
-                live["p_rstd", g, t], live["p_shift", g, t] = rstd, shift
+                nc.vector.scalar_tensor_tensor(
+                    out=blended[:, t, :], in0=live["h", g][:, t, :], scalar=2.0, in1=gated[:, t, :],
+                    op0=ALU.mult, op1=ALU.add, accum_out=sum_p[:, t : t + 1],
+                )
+            live["p", g], live["sum_p", g] = blended, sum_p
+
+        def blend_mean(g):
+            neg_mean = hold.tile([P, SUB], F32, name="p_neg_mean")
+            nc.scalar.mul(out=neg_mean[:], in_=live["sum_p", g][:], mul=-1.0 / H)
+            live["p_neg_mean", g] = neg_mean
+
+        def squared_deviations(v, neg_mean, sum_sq, width):
+            for t in range(SUB):
+                squares = early.tile([P, width], BF16, bufs=4)
+                nc.scalar.activation(
+                    out=squares[:], in_=v[:, t, :], func=ACT.Square, bias=neg_mean[:, t : t + 1], scale=1.0,
+                    accum_out=sum_sq[:, t : t + 1],
+                )
+
+        def blend_variance(g):
+            sum_sq = hold.tile([P, SUB], F32, name="p_sum_sq")
+            squared_deviations(live["p", g], live["p_neg_mean", g], sum_sq, H)
+            live["p_sum_sq", g] = sum_sq
+
+        def deviation(sum_sq, width):
+            std = stat.tile([P, SUB], F32)
+            nc.scalar.activation(out=std[:], in_=sum_sq[:], func=ACT.Sqrt, scale=1.0 / width, bias=eps_col[:])
+            return std
+
+        def blend_deviation(g):
+            live["p_std", g] = deviation(live["p_sum_sq", g], H)
+
+        def blend_scale(g):
+            rstd = stat.tile([P, SUB], F32, name="p_rstd")
+            nc.vector.reciprocal(out=rstd[:], in_=live["p_std", g][:])
+            shift = stat.tile([P, SUB], F32, name="p_shift")
+            nc.vector.tensor_tensor(out=shift[:], in0=live["p_neg_mean", g][:], in1=rstd[:], op=ALU.mult)
+            live["p_rstd", g], live["p_shift", g] = rstd, shift
 
         def normalise(g):
-            normed = work.tile([P, SUB, H], F32)
+            normed = late.tile([P, SUB, H], F32)
             for t in range(SUB):
                 nc.scalar.activation(
-                    out=normed[:, t, :], in_=live["p", g, t][:], func=ACT.Identity,
-                    scale=live["p_rstd", g, t][:], bias=live["p_shift", g, t][:],
+                    out=normed[:, t, :], in_=live["p", g][:, t, :], func=ACT.Identity,
+                    scale=live["p_rstd", g][:, t : t + 1], bias=live["p_shift", g][:, t : t + 1],
                 )
             live["normed", g] = normed
 
@@ -252,7 +255,7 @@ def tile_recurrentffn_pb_t_kernel(
                 live["nT", g, b] = nT
 
         def apply_gain(g):
-            nhT = work.tile([P, CHUNKS, TOK], F32)
+            nhT = late.tile([P, CHUNKS, TOK], F32)
             for b in range(CHUNKS // CPB):
                 for i in range(CPB):
                     m = b * CPB + i
@@ -262,13 +265,17 @@ def tile_recurrentffn_pb_t_kernel(
                     )
             live["nhT", g] = nhT
 
-        def quantise_state(g):
-            nh_quads = work.tile([P, TOK, PACK], BF16, align_bytes=64)
+        def group_state(g):
+            nh_quads = late.tile([P, TOK, PACK], BF16, align_bytes=64)
             nc.vector.tensor_copy(out=nh_quads[:], in_=live["nhT", g][:].rearrange("j m k -> j k m"))
-            nh_codes = work.tile([P, TOK], U32, align_bytes=64)
-            nh_scales = work.tile([P, TOK], U8, align_bytes=64)
+            live["nh_quads", g] = nh_quads
+
+        def quantise_state(g):
+            nh_codes = late.tile([P, TOK], U32, align_bytes=64)
+            nh_scales = late.tile([P, TOK], U8, align_bytes=64)
             nc.vector.quantize_mx(
-                out=nh_codes[:].bitcast(FP8X4), scales=nh_scales[:], in_=nh_quads[:].rearrange("j k m -> j (k m)")
+                out=nh_codes[:].bitcast(FP8X4), scales=nh_scales[:],
+                in_=live["nh_quads", g][:].rearrange("j k m -> j (k m)"),
             )
             live["nh_codes", g], live["nh_scales", g] = nh_codes, nh_scales
 
@@ -282,12 +289,13 @@ def tile_recurrentffn_pb_t_kernel(
                 live["nh", g, t] = nh_ps
 
         def store_state(g):
-            nh_rows = work.tile([P, SUB, H], F32, bufs=3)
+            nh_rows = late.tile([P, SUB, H], F32)
             for t in range(SUB):
                 nc.scalar.copy(out=nh_rows[:, t, :], in_=live["nh", g, t][:])
             nc.sync.dma_start(out=newh_v[:, group_rows(g), :], in_=nh_rows[:])
 
         def output_matmul(g):
+            wd_codes, wd_scales = live["wd"]
             for t in range(SUB):
                 y_ps = psum.tile([P, D], F32, tag="bank")
                 nc.tensor.matmul_mx(
@@ -302,31 +310,45 @@ def tile_recurrentffn_pb_t_kernel(
                 live["y", g, t] = y_ps
 
         def add_bias(g):
+            biased = late.tile([P, SUB, D], F32, bufs=4)
+            sum_y = stat.tile([P, SUB], F32)
             for t in range(SUB):
-                biased = rows.tile([P, D], F32, bufs=2 * SUB + 1)
-                sum_y = stat.tile([P, 1], F32)
                 nc.vector.scalar_tensor_tensor(
-                    out=biased[:], in0=live["y", g, t][:], scalar=1.0, in1=bd_all[:],
-                    op0=ALU.mult, op1=ALU.add, accum_out=sum_y[:],
+                    out=biased[:, t, :], in0=live["y", g, t][:], scalar=1.0, in1=bd_all[:],
+                    op0=ALU.mult, op1=ALU.add, accum_out=sum_y[:, t : t + 1],
                 )
-                live["yb", g, t] = biased
-                live["y_neg_mean", g, t] = negative_mean(sum_y, D)
+            live["yb", g], live["sum_y", g] = biased, sum_y
 
-        def second_variance(g):
-            for t in range(SUB):
-                live["y_rstd", g, t] = inverse_deviation(live["yb", g, t], live["y_neg_mean", g, t], D)
+        def output_mean(g):
+            neg_mean = stat.tile([P, SUB], F32, name="y_neg_mean")
+            nc.scalar.mul(out=neg_mean[:], in_=live["sum_y", g][:], mul=-1.0 / D)
+            live["y_neg_mean", g] = neg_mean
 
-        def finish_output(g):
-            out_rows = work.tile([P, SUB, D], F32, bufs=3)
+        def output_variance(g):
+            sum_sq = stat.tile([P, SUB], F32, name="y_sum_sq")
+            squared_deviations(live["yb", g], live["y_neg_mean", g], sum_sq, D)
+            live["y_sum_sq", g] = sum_sq
+
+        def output_deviation(g):
+            live["y_std", g] = deviation(live["y_sum_sq", g], D)
+
+        def output_gain(g):
+            rstd = stat.tile([P, SUB], F32, name="y_rstd")
+            nc.vector.reciprocal(out=rstd[:], in_=live["y_std", g][:])
+            gained = late.tile([P, SUB, D], F32)
             for t in range(SUB):
-                gained = rows.tile([P, D], F32)
                 nc.vector.scalar_tensor_tensor(
-                    out=gained[:], in0=live["yb", g, t][:], scalar=live["y_neg_mean", g, t][:], in1=go_all[:],
-                    op0=ALU.add, op1=ALU.mult,
+                    out=gained[:, t, :], in0=live["yb", g][:, t, :], scalar=live["y_neg_mean", g][:, t : t + 1],
+                    in1=go_all[:], op0=ALU.add, op1=ALU.mult,
                 )
+            live["y_rstd", g], live["gained", g] = rstd, gained
+
+        def output_shift(g):
+            out_rows = late.tile([P, SUB, D], F32)
+            for t in range(SUB):
                 nc.vector.scalar_tensor_tensor(
-                    out=out_rows[:, t, :], in0=gained[:], scalar=live["y_rstd", g, t][:], in1=bo_all[:],
-                    op0=ALU.mult, op1=ALU.add,
+                    out=out_rows[:, t, :], in0=live["gained", g][:, t, :], scalar=live["y_rstd", g][:, t : t + 1],
+                    in1=bo_all[:], op0=ALU.mult, op1=ALU.add,
                 )
             nc.sync.dma_start(out=out_v[:, group_rows(g), :], in_=out_rows[:])
 
@@ -334,24 +356,35 @@ def tile_recurrentffn_pb_t_kernel(
             if 0 <= g < GROUPS:
                 stage(g)
 
-        for s in range(-1, GROUPS + 3):
+        for s in range(-1, 2 * GROUPS + 5):
+            r = s - (GROUPS + 1)
             on(load_inputs, s + LOOKAHEAD)
-            on(copy_inputs_out, s)
-            on(blend, s - 1)
-            on(turn_normed, s - 2)
-            on(apply_gain, s - 2)
-            on(quantise_inputs, s)
-            on(turn_state_back, s - 2)
-            on(quantise_state, s - 2)
-            on(second_variance, s - 3)
-            on(gate_matmul, s)
-            on(difference, s + 1)
-            on(first_variance, s - 1)
-            on(output_matmul, s - 2)
-            on(store_state, s - 2)
-            on(finish_output, s - 3)
             on(turn_inputs, s + 1)
-            on(gate_sigmoid, s)
-            on(add_bias, s - 2)
-            on(turn_gate_back, s)
-            on(normalise, s - 1)
+            on(blend_mean, s - 3)
+            on(copy_inputs_out, s)
+            on(blend, s - 2)
+            on(gate_sigmoid, s - 1)
+            on(turn_gate_back, s - 1)
+            on(quantise_inputs, s)
+            on(gate_matmul, s)
+            on(blend_variance, s - 3)
+            on(difference, s + 1)
+            if s == GROUPS:
+                live["wd"] = quantise_weight(nc, late, keep, wd_raw, 1, D, "wd")
+
+            on(blend_deviation, r + 1)
+            on(output_mean, r - 3)
+            on(output_gain, r - 4)
+            on(normalise, r)
+            on(turn_normed, r)
+            on(add_bias, r - 2)
+            on(apply_gain, r - 1)
+            on(turn_state_back, r - 1)
+            on(group_state, r - 1)
+            on(output_variance, r - 3)
+            on(output_shift, r - 4)
+            on(store_state, r - 1)
+            on(quantise_state, r - 1)
+            on(output_matmul, r - 1)
+            on(output_deviation, r - 3)
+            on(blend_scale, r + 1)

@@ -57,49 +57,64 @@ def tile_recurrentffn_pb_t_kernel(
         inp = ctx.enter_context(tc.tile_pool(name="inp", bufs=4))
         early = ctx.enter_context(tc.tile_pool(name="early", bufs=2))
         stat = ctx.enter_context(tc.tile_pool(name="stat", bufs=8))
-        psum = ctx.enter_context(tc.psum_pool(name="psum", bufs=8))
+        psum = ctx.enter_context(tc.psum_pool(name="psum", bufs=6))
 
         live = {}
 
         def group_rows(g):
             return slice(g * SUB, (g + 1) * SUB)
 
-        def load_inputs(g):
-            x_sb = inp.tile([P, SUB, D], BF16)
+        def load_gate_inputs(g):
+            x_sb = inp.tile([P, SUB, D], BF16, bufs=3)
             nc.sync.dma_start(out=x_sb[:], in_=x_v[:, group_rows(g), :])
             h_sb = inp.tile([P, SUB, H], BF16, bufs=6)
             nc.sync.dma_start(out=h_sb[:], in_=h_v[:, group_rows(g), :])
-            s_sb = inp.tile([P, SUB, H], BF16)
+            live["x", g], live["h", g] = x_sb, h_sb
+
+        def load_candidate(g):
+            s_sb = inp.tile([P, SUB, H], BF16, bufs=4)
             nc.sync.dma_start(out=s_sb[:], in_=s_v[:, group_rows(g), :])
-            live["x", g], live["h", g], live["s", g] = x_sb, h_sb, s_sb
+            live["s", g] = s_sb
 
         ident = keep.tile([P, P], F32)
         make_identity(nc, ident[:])
         eps_col = keep.tile([P, 1], F32)
         nc.gpsimd.memset(eps_col[:], EPS)
 
+        def turn_inputs(g):
+            for t in range(SUB):
+                xhT = psum.tile([P, 2, 2, P], F32, tag="bank")
+                for c, src in enumerate((live["x", g], live["h", g])):
+                    src_words = src[:, t, :].bitcast(F32)
+                    for u in range(2):
+                        nc.tensor.transpose(xhT[:, c, u, :], src_words[:, u * P : (u + 1) * P], ident[:])
+                live["xhT", g, t] = xhT
+
         with tc.tile_pool(name="prep", bufs=1) as prep:
+            load_gate_inputs(0)
             wu_raw = prep.tile([P, 2, PACK, H], BF16)
-            nc.sync.dma_start(
-                out=wu_raw[:].rearrange("p c (u e) n -> p (c u) (e n)", e=2),
-                in_=W_u.rearrange("(cu p e) n -> p cu (e n)", p=P, e=2),
-            )
-            for g in range(LOOKAHEAD - 1):
-                load_inputs(g)
+            wu_v = W_u.rearrange("(c u p e) n -> c p u (e n)", c=2, p=P, e=2)
+            for c in range(2):
+                nc.sync.dma_start(out=wu_raw[:, c].rearrange("p (u e) n -> p u (e n)", e=2), in_=wu_v[c])
+            load_candidate(0)
+            for g in range(1, LOOKAHEAD):
+                load_gate_inputs(g)
+                load_candidate(g)
+            turn_inputs(0)
 
             vec_rows = prep.tile([P, P], BF16)
-            nc.vector.memset(vec_rows[:], 0.0)
+            nc.gpsimd.memset(vec_rows[:], 0.0)
             for v, vec in enumerate((b_u, gamma_h, beta_h)):
                 nc.scalar.dma_start(
                     out=vec_rows[v * CHUNKS : (v + 1) * CHUNKS, :], in_=vec.rearrange("(m j) -> m j", j=P)
                 )
             vec_rows_f32 = prep.tile([P, P], F32)
-            nc.vector.tensor_copy(out=vec_rows_f32[:], in_=vec_rows[:])
+            nc.gpsimd.tensor_copy(out=vec_rows_f32[:], in_=vec_rows[:])
             vec_cols_ps = psum.tile([P, P], F32, tag="bank")
             nc.tensor.transpose(vec_cols_ps[:], vec_rows_f32[:], ident[:])
+            wu_codes, wu_scales = quantise_weight(nc, prep, keep, wu_raw, 2, H, "wu")
             vec_cols = keep.tile([P, 3 * CHUNKS], F32)
             nc.vector.tensor_copy(out=vec_cols[:], in_=vec_cols_ps[:, : 3 * CHUNKS])
-            wu_codes, wu_scales = quantise_weight(nc, prep, keep, wu_raw, 2, H, "wu")
 
         def column(v, m):
             return vec_cols[:, v * CHUNKS + m : v * CHUNKS + m + 1]
@@ -110,19 +125,20 @@ def tile_recurrentffn_pb_t_kernel(
         nc.gpsimd.dma_start(out=wd_raw[:, 0], in_=W_d.rearrange("(m p) n -> p m n", p=P))
         bd_all = keep.tile([P, D], BF16)
         nc.gpsimd.dma_start(out=bd_all[:], in_=b_d.partition_broadcast(P))
-        go_all = keep.tile([P, D], BF16)
-        nc.gpsimd.dma_start(out=go_all[:], in_=gamma_o.partition_broadcast(P))
-        bo_all = keep.tile([P, D], BF16)
-        nc.gpsimd.dma_start(out=bo_all[:], in_=beta_o.partition_broadcast(P))
+        ones = keep.tile([P, P], BF16)
+        nc.gpsimd.memset(ones[:], 1.0)
+        first_rows = late.tile([P, 2, D], BF16, bufs=1)
+        nc.gpsimd.memset(first_rows[:], 0.0)
+        nc.gpsimd.dma_start(out=first_rows[0:1, 0, :], in_=gamma_o.rearrange("(o d) -> o d", o=1))
+        nc.gpsimd.dma_start(out=first_rows[0:1, 1, :], in_=beta_o.rearrange("(o d) -> o d", o=1))
 
-        def turn_inputs(g):
-            for t in range(SUB):
-                xhT = psum.tile([P, 2, 2, P], F32, tag="bank")
-                for c, src in enumerate((live["x", g], live["h", g])):
-                    src_words = src[:, t, :].bitcast(F32)
-                    for u in range(2):
-                        nc.tensor.transpose(xhT[:, c, u, :], src_words[:, u * P : (u + 1) * P], ident[:])
-                live["xhT", g, t] = xhT
+        def prepare_second_half():
+            live["wd"] = quantise_weight(nc, late, keep, wd_raw, 1, D, "wd")
+            go_all = psum.tile([P, D], F32, bufs=1)
+            nc.tensor.matmul(out=go_all[:], lhsT=ones[:], rhs=first_rows[:, 0, :], start=True, stop=True)
+            bo_all = psum.tile([P, D], F32, bufs=1)
+            nc.tensor.matmul(out=bo_all[:], lhsT=ones[:], rhs=first_rows[:, 1, :], start=True, stop=True)
+            live["go_all"], live["bo_all"] = go_all, bo_all
 
         def copy_inputs_out(g):
             xh_quads = early.tile([P, 2 * TOK * PACK], BF16, align_bytes=64)
@@ -182,7 +198,7 @@ def tile_recurrentffn_pb_t_kernel(
                 live["u", g, t] = u_ps
 
         def difference(g):
-            diff = early.tile([P, SUB, H], F32, bufs=4)
+            diff = early.tile([P, SUB, H], F32, bufs=3)
             nc.vector.tensor_tensor(out=diff[:], in0=live["s", g][:], in1=live["h", g][:], op=ALU.subtract)
             live["diff", g] = diff
 
@@ -208,7 +224,7 @@ def tile_recurrentffn_pb_t_kernel(
 
         def squared_deviations(v, neg_mean, sum_sq, width):
             for t in range(SUB):
-                squares = early.tile([P, width], BF16, bufs=4)
+                squares = early.tile([P, width], BF16)
                 nc.scalar.activation(
                     out=squares[:], in_=v[:, t, :], func=ACT.Square, bias=neg_mean[:, t : t + 1], scale=1.0,
                     accum_out=sum_sq[:, t : t + 1],
@@ -237,9 +253,10 @@ def tile_recurrentffn_pb_t_kernel(
         def normalise(g):
             normed = late.tile([P, SUB, H], F32)
             for t in range(SUB):
-                nc.scalar.activation(
-                    out=normed[:, t, :], in_=live["p", g][:, t, :], func=ACT.Identity,
-                    scale=live["p_rstd", g][:, t : t + 1], bias=live["p_shift", g][:, t : t + 1],
+                nc.gpsimd.tensor_scalar(
+                    out=normed[:, t, :], in0=live["p", g][:, t, :],
+                    scalar1=live["p_rstd", g][:, t : t + 1], scalar2=live["p_shift", g][:, t : t + 1],
+                    op0=ALU.mult, op1=ALU.add,
                 )
             live["normed", g] = normed
 
@@ -255,7 +272,7 @@ def tile_recurrentffn_pb_t_kernel(
                 live["nT", g, b] = nT
 
         def apply_gain(g):
-            nhT = late.tile([P, CHUNKS, TOK], F32)
+            nhT = late.tile([P, CHUNKS, TOK], F32, bufs=4)
             for b in range(CHUNKS // CPB):
                 for i in range(CPB):
                     m = b * CPB + i
@@ -267,7 +284,10 @@ def tile_recurrentffn_pb_t_kernel(
 
         def group_state(g):
             nh_quads = late.tile([P, TOK, PACK], BF16, align_bytes=64)
-            nc.vector.tensor_copy(out=nh_quads[:], in_=live["nhT", g][:].rearrange("j m k -> j k m"))
+            nc.gpsimd.tensor_scalar(
+                out=nh_quads[:], in0=live["nhT", g][:].rearrange("j m k -> j k m"),
+                scalar1=1.0, scalar2=0.0, op0=ALU.mult, op1=ALU.add,
+            )
             live["nh_quads", g] = nh_quads
 
         def quantise_state(g):
@@ -292,7 +312,7 @@ def tile_recurrentffn_pb_t_kernel(
             nh_rows = late.tile([P, SUB, H], F32)
             for t in range(SUB):
                 nc.scalar.copy(out=nh_rows[:, t, :], in_=live["nh", g, t][:])
-            nc.sync.dma_start(out=newh_v[:, group_rows(g), :], in_=nh_rows[:])
+                nc.sync.dma_start(out=newh_v[:, g * SUB + t, :], in_=nh_rows[:, t, :])
 
         def output_matmul(g):
             wd_codes, wd_scales = live["wd"]
@@ -310,7 +330,7 @@ def tile_recurrentffn_pb_t_kernel(
                 live["y", g, t] = y_ps
 
         def add_bias(g):
-            biased = late.tile([P, SUB, D], F32, bufs=4)
+            biased = late.tile([P, SUB, D], F32, bufs=3)
             sum_y = stat.tile([P, SUB], F32)
             for t in range(SUB):
                 nc.vector.scalar_tensor_tensor(
@@ -332,59 +352,64 @@ def tile_recurrentffn_pb_t_kernel(
         def output_deviation(g):
             live["y_std", g] = deviation(live["y_sum_sq", g], D)
 
-        def output_gain(g):
+        def output_scale(g):
             rstd = stat.tile([P, SUB], F32, name="y_rstd")
             nc.vector.reciprocal(out=rstd[:], in_=live["y_std", g][:])
+            live["y_rstd", g] = rstd
+
+        def output_gain(g):
             gained = late.tile([P, SUB, D], F32)
             for t in range(SUB):
                 nc.vector.scalar_tensor_tensor(
                     out=gained[:, t, :], in0=live["yb", g][:, t, :], scalar=live["y_neg_mean", g][:, t : t + 1],
-                    in1=go_all[:], op0=ALU.add, op1=ALU.mult,
+                    in1=live["go_all"][:], op0=ALU.add, op1=ALU.mult,
                 )
-            live["y_rstd", g], live["gained", g] = rstd, gained
+            live["gained", g] = gained
 
         def output_shift(g):
             out_rows = late.tile([P, SUB, D], F32)
             for t in range(SUB):
                 nc.vector.scalar_tensor_tensor(
                     out=out_rows[:, t, :], in0=live["gained", g][:, t, :], scalar=live["y_rstd", g][:, t : t + 1],
-                    in1=bo_all[:], op0=ALU.mult, op1=ALU.add,
+                    in1=live["bo_all"][:], op0=ALU.mult, op1=ALU.add,
                 )
-            nc.sync.dma_start(out=out_v[:, group_rows(g), :], in_=out_rows[:])
+                nc.sync.dma_start(out=out_v[:, g * SUB + t, :], in_=out_rows[:, t, :])
 
         def on(stage, g):
             if 0 <= g < GROUPS:
                 stage(g)
 
-        for s in range(-1, 2 * GROUPS + 5):
+        for s in range(2 * GROUPS + 5):
             r = s - (GROUPS + 1)
-            on(load_inputs, s + LOOKAHEAD)
+            on(load_gate_inputs, s + LOOKAHEAD)
+            on(load_candidate, s + LOOKAHEAD)
             on(turn_inputs, s + 1)
-            on(blend_mean, s - 3)
             on(copy_inputs_out, s)
             on(blend, s - 2)
             on(gate_sigmoid, s - 1)
             on(turn_gate_back, s - 1)
             on(quantise_inputs, s)
             on(gate_matmul, s)
-            on(blend_variance, s - 3)
-            on(difference, s + 1)
-            if s == GROUPS:
-                live["wd"] = quantise_weight(nc, late, keep, wd_raw, 1, D, "wd")
+            on(difference, s)
+            on(blend_mean, s - 2)
+            on(blend_variance, s - 2)
 
+            if r == 1:
+                prepare_second_half()
             on(blend_deviation, r + 1)
-            on(output_mean, r - 3)
-            on(output_gain, r - 4)
+            on(output_scale, r - 4)
             on(normalise, r)
-            on(turn_normed, r)
-            on(add_bias, r - 2)
+            on(quantise_state, r - 2)
+            on(output_matmul, r - 2)
             on(apply_gain, r - 1)
-            on(turn_state_back, r - 1)
-            on(group_state, r - 1)
-            on(output_variance, r - 3)
             on(output_shift, r - 4)
-            on(store_state, r - 1)
-            on(quantise_state, r - 1)
-            on(output_matmul, r - 1)
+            on(turn_normed, r)
+            on(group_state, r - 1)
+            on(store_state, r - 4)
+            on(add_bias, r - 2)
+            on(turn_state_back, r - 3)
+            on(output_mean, r - 3)
+            on(output_variance, r - 3)
+            on(output_gain, r - 3)
             on(output_deviation, r - 3)
             on(blend_scale, r + 1)

@@ -57,7 +57,7 @@ def tile_recurrentffn_pb_t_kernel(
         inp = ctx.enter_context(tc.tile_pool(name="inp", bufs=4))
         early = ctx.enter_context(tc.tile_pool(name="early", bufs=2))
         stat = ctx.enter_context(tc.tile_pool(name="stat", bufs=8))
-        psum = ctx.enter_context(tc.psum_pool(name="psum", bufs=6))
+        psum = ctx.enter_context(tc.psum_pool(name="psum", bufs=8))
 
         live = {}
 
@@ -105,7 +105,7 @@ def tile_recurrentffn_pb_t_kernel(
             vec_rows = prep.tile([P, P], BF16)
             nc.gpsimd.memset(vec_rows[:], 0.0)
             for v, vec in enumerate((b_u, gamma_h, beta_h)):
-                nc.scalar.dma_start(
+                nc.gpsimd.dma_start(
                     out=vec_rows[v * CHUNKS : (v + 1) * CHUNKS, :], in_=vec.rearrange("(m j) -> m j", j=P)
                 )
             vec_rows_f32 = prep.tile([P, P], F32)
@@ -134,9 +134,9 @@ def tile_recurrentffn_pb_t_kernel(
 
         def prepare_second_half():
             live["wd"] = quantise_weight(nc, late, keep, wd_raw, 1, D, "wd")
-            go_all = psum.tile([P, D], F32, bufs=1)
+            go_all = psum.tile([P, D], F32, tag="bank")
             nc.tensor.matmul(out=go_all[:], lhsT=ones[:], rhs=first_rows[:, 0, :], start=True, stop=True)
-            bo_all = psum.tile([P, D], F32, bufs=1)
+            bo_all = psum.tile([P, D], F32, tag="bank")
             nc.tensor.matmul(out=bo_all[:], lhsT=ones[:], rhs=first_rows[:, 1, :], start=True, stop=True)
             live["go_all"], live["bo_all"] = go_all, bo_all
 
@@ -199,7 +199,11 @@ def tile_recurrentffn_pb_t_kernel(
 
         def difference(g):
             diff = early.tile([P, SUB, H], F32, bufs=3)
-            nc.vector.tensor_tensor(out=diff[:], in0=live["s", g][:], in1=live["h", g][:], op=ALU.subtract)
+            for t in range(SUB):
+                engine = nc.vector if t % 2 == 0 else nc.gpsimd
+                engine.tensor_tensor(
+                    out=diff[:, t, :], in0=live["s", g][:, t, :], in1=live["h", g][:, t, :], op=ALU.subtract
+                )
             live["diff", g] = diff
 
         def blend(g):
@@ -383,33 +387,33 @@ def tile_recurrentffn_pb_t_kernel(
             r = s - (GROUPS + 1)
             on(load_gate_inputs, s + LOOKAHEAD)
             on(load_candidate, s + LOOKAHEAD)
+            on(turn_gate_back, s - 2)
+            on(gate_matmul, s - 1)
             on(turn_inputs, s + 1)
             on(copy_inputs_out, s)
-            on(blend, s - 2)
-            on(gate_sigmoid, s - 1)
-            on(turn_gate_back, s - 1)
-            on(quantise_inputs, s)
-            on(gate_matmul, s)
             on(difference, s)
-            on(blend_mean, s - 2)
-            on(blend_variance, s - 2)
+            on(blend, s - 2)
+            on(blend_mean, s - 3)
+            on(blend_variance, s - 3)
+            on(quantise_inputs, s)
+            on(gate_sigmoid, s - 1)
 
             if r == 1:
                 prepare_second_half()
             on(blend_deviation, r + 1)
+            on(output_mean, r - 3)
             on(output_scale, r - 4)
             on(normalise, r)
             on(quantise_state, r - 2)
             on(output_matmul, r - 2)
             on(apply_gain, r - 1)
             on(output_shift, r - 4)
+            on(blend_scale, r + 1)
             on(turn_normed, r)
             on(group_state, r - 1)
             on(store_state, r - 4)
             on(add_bias, r - 2)
             on(turn_state_back, r - 3)
-            on(output_mean, r - 3)
             on(output_variance, r - 3)
             on(output_gain, r - 3)
             on(output_deviation, r - 3)
-            on(blend_scale, r + 1)

@@ -199,11 +199,7 @@ def tile_recurrentffn_pb_t_kernel(
 
         def difference(g):
             diff = early.tile([P, SUB, H], F32, bufs=3)
-            for t in range(SUB):
-                engine = nc.vector if t % 2 == 0 else nc.gpsimd
-                engine.tensor_tensor(
-                    out=diff[:, t, :], in0=live["s", g][:, t, :], in1=live["h", g][:, t, :], op=ALU.subtract
-                )
+            nc.vector.tensor_tensor(out=diff[:], in0=live["s", g][:], in1=live["h", g][:], op=ALU.subtract)
             live["diff", g] = diff
 
         def blend(g):

from contextlib import ExitStack

import concourse.mybir as mybir
from concourse.masks import make_identity

F32 = mybir.dt.float32
BF16 = mybir.dt.bfloat16
U32 = mybir.dt.uint32
U8 = mybir.dt.uint8
FP8X4 = mybir.dt.float8_e4m3fn_x4
ALU = mybir.AluOpType
ACT = mybir.ActivationFunctionType

P = 128
PACK = 4
B, D, H = 4096, 512, 512
EPS = 1e-3
CHUNKS = H // P
SUB = 2
TOK = SUB * P
GROUPS = B // TOK
BANK = 512
CPB = BANK // TOK
LOOKAHEAD = 3

FLOPS = 2 * B * (D + H) * H + 2 * B * H * D


def quantise_weight(nc, pool, keep, raw, passes, width, label):
    quads = pool.tile([P, passes, width, PACK], BF16, align_bytes=64, name=label + "_quads", bufs=1)
    for c in range(passes):
        nc.vector.tensor_copy(out=quads[:, c], in_=raw[:, c].rearrange("p t n -> p n t"))
    codes = keep.tile([P, passes, width], U32, align_bytes=64, name=label + "_codes")
    scales = keep.tile([P, passes, width], U8, align_bytes=64, name=label + "_scales")
    nc.vector.quantize_mx(
        out=codes[:].rearrange("p c n -> p (c n)").bitcast(FP8X4),
        scales=scales[:].rearrange("p c n -> p (c n)"),
        in_=quads[:].rearrange("p c n t -> p (c n t)"),
    )
    return codes, scales


def tile_recurrentffn_pb_t_kernel(
    tc, x, hidden_state, swiglu, W_u, b_u, gamma_h, beta_h, W_d, b_d, gamma_o, beta_o, out_0, out_1
):
    nc = tc.nc
    x_v = x.rearrange("(p j) d -> p j d", p=P)
    h_v = hidden_state.rearrange("(p j) d -> p j d", p=P)
    s_v = swiglu.rearrange("(p j) d -> p j d", p=P)
    out_v = out_0.rearrange("(p j) d -> p j d", p=P)
    newh_v = out_1.rearrange("(p j) d -> p j d", p=P)

    with ExitStack() as ctx:
        ctx.enter_context(tc.manual_schedule())
        keep = ctx.enter_context(tc.tile_pool(name="keep", bufs=1))
        hold = ctx.enter_context(tc.tile_pool(name="hold", bufs=GROUPS))
        inp = ctx.enter_context(tc.tile_pool(name="inp", bufs=4))
        early = ctx.enter_context(tc.tile_pool(name="early", bufs=2))
        stat = ctx.enter_context(tc.tile_pool(name="stat", bufs=8))
        psum = ctx.enter_context(tc.psum_pool(name="psum", bufs=8))

        live = {}

        def group_rows(g):
            return slice(g * SUB, (g + 1) * SUB)

        def load_gate_inputs(g):
            x_sb = inp.tile([P, SUB, D], BF16, bufs=3)
            nc.sync.dma_start(out=x_sb[:], in_=x_v[:, group_rows(g), :])
            h_sb = inp.tile([P, SUB, H], BF16, bufs=6)
            nc.sync.dma_start(out=h_sb[:], in_=h_v[:, group_rows(g), :])
            live["x", g], live["h", g] = x_sb, h_sb

        def load_candidate(g):
            s_sb = inp.tile([P, SUB, H], BF16, bufs=4)
            nc.sync.dma_start(out=s_sb[:], in_=s_v[:, group_rows(g), :])
            live["s", g] = s_sb

        ident = keep.tile([P, P], F32)
        make_identity(nc, ident[:])
        eps_col = keep.tile([P, 1], F32)
        nc.gpsimd.memset(eps_col[:], EPS)

        def turn_inputs(g):
            for t in range(SUB):
                xhT = psum.tile([P, 2, 2, P], F32, tag="bank")
                for c, src in enumerate((live["x", g], live["h", g])):
                    src_words = src[:, t, :].bitcast(F32)
                    for u in range(2):
                        nc.tensor.transpose(xhT[:, c, u, :], src_words[:, u * P : (u + 1) * P], ident[:])
                live["xhT", g, t] = xhT

        with tc.tile_pool(name="prep", bufs=1) as prep:
            load_gate_inputs(0)
            wu_raw = prep.tile([P, 2, PACK, H], BF16)
            wu_v = W_u.rearrange("(c u p e) n -> c p u (e n)", c=2, p=P, e=2)
            for c in range(2):
                nc.sync.dma_start(out=wu_raw[:, c].rearrange("p (u e) n -> p u (e n)", e=2), in_=wu_v[c])
            load_candidate(0)
            for g in range(1, LOOKAHEAD):
                load_gate_inputs(g)
                load_candidate(g)
            turn_inputs(0)

            vec_rows = prep.tile([P, P], BF16)
            nc.gpsimd.memset(vec_rows[:], 0.0)
            for v, vec in enumerate((b_u, gamma_h, beta_h)):
                nc.gpsimd.dma_start(
                    out=vec_rows[v * CHUNKS : (v + 1) * CHUNKS, :], in_=vec.rearrange("(m j) -> m j", j=P)
                )
            vec_rows_f32 = prep.tile([P, P], F32)
            nc.gpsimd.tensor_copy(out=vec_rows_f32[:], in_=vec_rows[:])
            vec_cols_ps = psum.tile([P, P], F32, tag="bank")
            nc.tensor.transpose(vec_cols_ps[:], vec_rows_f32[:], ident[:])
            wu_codes, wu_scales = quantise_weight(nc, prep, keep, wu_raw, 2, H, "wu")
            vec_cols = keep.tile([P, 3 * CHUNKS], F32)
            nc.vector.tensor_copy(out=vec_cols[:], in_=vec_cols_ps[:, : 3 * CHUNKS])

        def column(v, m):
            return vec_cols[:, v * CHUNKS + m : v * CHUNKS + m + 1]

        late = ctx.enter_context(tc.tile_pool(name="late", bufs=2))

        wd_raw = late.tile([P, 1, PACK, D], BF16, bufs=1)
        nc.gpsimd.dma_start(out=wd_raw[:, 0], in_=W_d.rearrange("(m p) n -> p m n", p=P))
        bd_all = keep.tile([P, D], BF16)
        nc.gpsimd.dma_start(out=bd_all[:], in_=b_d.partition_broadcast(P))
        ones = keep.tile([P, P], BF16)
        nc.gpsimd.memset(ones[:], 1.0)
        first_rows = late.tile([P, 2, D], BF16, bufs=1)
        nc.gpsimd.memset(first_rows[:], 0.0)
        nc.gpsimd.dma_start(out=first_rows[0:1, 0, :], in_=gamma_o.rearrange("(o d) -> o d", o=1))
        nc.gpsimd.dma_start(out=first_rows[0:1, 1, :], in_=beta_o.rearrange("(o d) -> o d", o=1))

        def prepare_second_half():
            live["wd"] = quantise_weight(nc, late, keep, wd_raw, 1, D, "wd")
            go_all = psum.tile([P, D], F32, tag="bank")
            nc.tensor.matmul(out=go_all[:], lhsT=ones[:], rhs=first_rows[:, 0, :], start=True, stop=True)
            bo_all = psum.tile([P, D], F32, tag="bank")
            nc.tensor.matmul(out=bo_all[:], lhsT=ones[:], rhs=first_rows[:, 1, :], start=True, stop=True)
            live["go_all"], live["bo_all"] = go_all, bo_all

        def copy_inputs_out(g):
            xh_quads = early.tile([P, 2 * TOK * PACK], BF16, align_bytes=64)
            xh_words = xh_quads[:].bitcast(F32).rearrange("q (c k u) -> q c k u", c=2, u=2)
            for t in range(SUB):
                nc.scalar.copy(
                    out=xh_words[:, :, t * P : (t + 1) * P, :],
                    in_=live["xhT", g, t][:].rearrange("q c u k -> q c k u"),
                )
            live["xh_quads", g] = xh_quads

        def quantise_inputs(g):
            xh_codes = early.tile([P, 2, TOK], U32, align_bytes=64)
            xh_scales = early.tile([P, 2, TOK], U8, align_bytes=64)
            nc.vector.quantize_mx(
                out=xh_codes[:].rearrange("q c k -> q (c k)").bitcast(FP8X4),
                scales=xh_scales[:].rearrange("q c k -> q (c k)"),
                in_=live["xh_quads", g][:],
            )
            live["xh_codes", g], live["xh_scales", g] = xh_codes, xh_scales

        def gate_matmul(g):
            for b in range(CHUNKS // CPB):
                zT = psum.tile([P, CPB, TOK], F32, tag="bank")
                for i in range(CPB):
                    m = b * CPB + i
                    for c in range(2):
                        nc.tensor.matmul_mx(
                            out=zT[:, i, :],
                            lhsT=wu_codes[:, c, m * P : (m + 1) * P].bitcast(FP8X4),
                            lhsT_scale=wu_scales[:, c, m * P : (m + 1) * P],
                            rhs=live["xh_codes", g][:, c, :].bitcast(FP8X4),
                            rhs_scale=live["xh_scales", g][:, c, :],
                            start=(c == 0),
                            stop=(c == 1),
                        )
                live["zT", g, b] = zT

        def gate_sigmoid(g):
            uT = early.tile([P, CHUNKS, TOK], F32)
            for b in range(CHUNKS // CPB):
                for i in range(CPB):
                    m = b * CPB + i
                    nc.scalar.activation(
                        out=uT[:, m, :], in_=live["zT", g, b][:, i, :], func=ACT.Sigmoid,
                        bias=column(0, m), scale=1.0,
                    )
            live["uT", g] = uT

        def turn_gate_back(g):
            for t in range(SUB):
                u_ps = psum.tile([P, H], F32, tag="bank")
                for m in range(CHUNKS):
                    nc.tensor.transpose(
                        u_ps[:, m * P : (m + 1) * P], live["uT", g][:, m, t * P : (t + 1) * P], ident[:]
                    )
                live["u", g, t] = u_ps

        def difference(g):
            diff = early.tile([P, SUB, H], F32, bufs=3)
            nc.vector.tensor_tensor(out=diff[:], in0=live["s", g][:], in1=live["h", g][:], op=ALU.subtract)
            live["diff", g] = diff

        def blend(g):
            gated = early.tile([P, SUB, H], F32)
            blended = hold.tile([P, SUB, H], F32)
            sum_p = hold.tile([P, SUB], F32)
            for t in range(SUB):
                nc.vector.tensor_tensor(
                    out=gated[:, t, :], in0=live["u", g, t][:], in1=live["diff", g][:, t, :], op=ALU.mult
                )
            for t in range(SUB):
                nc.vector.scalar_tensor_tensor(
                    out=blended[:, t, :], in0=live["h", g][:, t, :], scalar=2.0, in1=gated[:, t, :],
                    op0=ALU.mult, op1=ALU.add, accum_out=sum_p[:, t : t + 1],
                )
            live["p", g], live["sum_p", g] = blended, sum_p

        def blend_mean(g):
            neg_mean = hold.tile([P, SUB], F32, name="p_neg_mean")
            nc.scalar.mul(out=neg_mean[:], in_=live["sum_p", g][:], mul=-1.0 / H)
            live["p_neg_mean", g] = neg_mean

        def squared_deviations(v, neg_mean, sum_sq, width):
            for t in range(SUB):
                squares = early.tile([P, width], BF16)
                nc.scalar.activation(
                    out=squares[:], in_=v[:, t, :], func=ACT.Square, bias=neg_mean[:, t : t + 1], scale=1.0,
                    accum_out=sum_sq[:, t : t + 1],
                )

        def blend_variance(g):
            sum_sq = hold.tile([P, SUB], F32, name="p_sum_sq")
            squared_deviations(live["p", g], live["p_neg_mean", g], sum_sq, H)
            live["p_sum_sq", g] = sum_sq

        def deviation(sum_sq, width):
            std = stat.tile([P, SUB], F32)
            nc.scalar.activation(out=std[:], in_=sum_sq[:], func=ACT.Sqrt, scale=1.0 / width, bias=eps_col[:])
            return std

        def blend_deviation(g):
            live["p_std", g] = deviation(live["p_sum_sq", g], H)

        def blend_scale(g):
            rstd = stat.tile([P, SUB], F32, name="p_rstd")
            nc.vector.reciprocal(out=rstd[:], in_=live["p_std", g][:])
            shift = stat.tile([P, SUB], F32, name="p_shift")
            nc.vector.tensor_tensor(out=shift[:], in0=live["p_neg_mean", g][:], in1=rstd[:], op=ALU.mult)
            live["p_rstd", g], live["p_shift", g] = rstd, shift

        def normalise(g):
            normed = late.tile([P, SUB, H], F32)
            for t in range(SUB):
                nc.gpsimd.tensor_scalar(
                    out=normed[:, t, :], in0=live["p", g][:, t, :],
                    scalar1=live["p_rstd", g][:, t : t + 1], scalar2=live["p_shift", g][:, t : t + 1],
                    op0=ALU.mult, op1=ALU.add,
                )
            live["normed", g] = normed

        def turn_normed(g):
            for b in range(CHUNKS // CPB):
                nT = psum.tile([P, CPB, TOK], F32, tag="bank")
                for i in range(CPB):
                    m = b * CPB + i
                    for t in range(SUB):
                        nc.tensor.transpose(
                            nT[:, i, t * P : (t + 1) * P], live["normed", g][:, t, m * P : (m + 1) * P], ident[:]
                        )
                live["nT", g, b] = nT

        def apply_gain(g):
            nhT = late.tile([P, CHUNKS, TOK], F32, bufs=4)
            for b in range(CHUNKS // CPB):
                for i in range(CPB):
                    m = b * CPB + i
                    nc.scalar.activation(
                        out=nhT[:, m, :], in_=live["nT", g, b][:, i, :], func=ACT.Identity,
                        scale=column(1, m), bias=column(2, m),
                    )
            live["nhT", g] = nhT

        def group_state(g):
            nh_quads = late.tile([P, TOK, PACK], BF16, align_bytes=64)
            nc.gpsimd.tensor_scalar(
                out=nh_quads[:], in0=live["nhT", g][:].rearrange("j m k -> j k m"),
                scalar1=1.0, scalar2=0.0, op0=ALU.mult, op1=ALU.add,
            )
            live["nh_quads", g] = nh_quads

        def quantise_state(g):
            nh_codes = late.tile([P, TOK], U32, align_bytes=64)
            nh_scales = late.tile([P, TOK], U8, align_bytes=64)
            nc.vector.quantize_mx(
                out=nh_codes[:].bitcast(FP8X4), scales=nh_scales[:],
                in_=live["nh_quads", g][:].rearrange("j k m -> j (k m)"),
            )
            live["nh_codes", g], live["nh_scales", g] = nh_codes, nh_scales

        def turn_state_back(g):
            for t in range(SUB):
                nh_ps = psum.tile([P, H], F32, tag="bank")
                for m in range(CHUNKS):
                    nc.tensor.transpose(
                        nh_ps[:, m * P : (m + 1) * P], live["nhT", g][:, m, t * P : (t + 1) * P], ident[:]
                    )
                live["nh", g, t] = nh_ps

        def store_state(g):
            nh_rows = late.tile([P, SUB, H], F32)
            for t in range(SUB):
                nc.scalar.copy(out=nh_rows[:, t, :], in_=live["nh", g, t][:])
                nc.sync.dma_start(out=newh_v[:, g * SUB + t, :], in_=nh_rows[:, t, :])

        def output_matmul(g):
            wd_codes, wd_scales = live["wd"]
            for t in range(SUB):
                y_ps = psum.tile([P, D], F32, tag="bank")
                nc.tensor.matmul_mx(
                    out=y_ps[:],
                    lhsT=live["nh_codes", g][:, t * P : (t + 1) * P].bitcast(FP8X4),
                    lhsT_scale=live["nh_scales", g][:, t * P : (t + 1) * P],
                    rhs=wd_codes[:, 0, :].bitcast(FP8X4),
                    rhs_scale=wd_scales[:, 0, :],
                    start=True,
                    stop=True,
                )
                live["y", g, t] = y_ps

        def add_bias(g):
            biased = late.tile([P, SUB, D], F32, bufs=3)
            sum_y = stat.tile([P, SUB], F32)
            for t in range(SUB):
                nc.vector.scalar_tensor_tensor(
                    out=biased[:, t, :], in0=live["y", g, t][:], scalar=1.0, in1=bd_all[:],
                    op0=ALU.mult, op1=ALU.add, accum_out=sum_y[:, t : t + 1],
                )
            live["yb", g], live["sum_y", g] = biased, sum_y

        def output_mean(g):
            neg_mean = stat.tile([P, SUB], F32, name="y_neg_mean")
            nc.scalar.mul(out=neg_mean[:], in_=live["sum_y", g][:], mul=-1.0 / D)
            live["y_neg_mean", g] = neg_mean

        def output_variance(g):
            sum_sq = stat.tile([P, SUB], F32, name="y_sum_sq")
            squared_deviations(live["yb", g], live["y_neg_mean", g], sum_sq, D)
            live["y_sum_sq", g] = sum_sq

        def output_deviation(g):
            live["y_std", g] = deviation(live["y_sum_sq", g], D)

        def output_scale(g):
            rstd = stat.tile([P, SUB], F32, name="y_rstd")
            nc.vector.reciprocal(out=rstd[:], in_=live["y_std", g][:])
            live["y_rstd", g] = rstd

        def output_gain(g):
            gained = late.tile([P, SUB, D], F32)
            for t in range(SUB):
                nc.vector.scalar_tensor_tensor(
                    out=gained[:, t, :], in0=live["yb", g][:, t, :], scalar=live["y_neg_mean", g][:, t : t + 1],
                    in1=live["go_all"][:], op0=ALU.add, op1=ALU.mult,
                )
            live["gained", g] = gained

        def output_shift(g):
            out_rows = late.tile([P, SUB, D], F32)
            for t in range(SUB):
                nc.vector.scalar_tensor_tensor(
                    out=out_rows[:, t, :], in0=live["gained", g][:, t, :], scalar=live["y_rstd", g][:, t : t + 1],
                    in1=live["bo_all"][:], op0=ALU.mult, op1=ALU.add,
                )
                nc.sync.dma_start(out=out_v[:, g * SUB + t, :], in_=out_rows[:, t, :])

        def on(stage, g):
            if 0 <= g < GROUPS:
                stage(g)

        for s in range(2 * GROUPS + 5):
            r = s - (GROUPS + 1)
            on(load_gate_inputs, s + LOOKAHEAD)
            on(load_candidate, s + LOOKAHEAD)
            on(turn_gate_back, s - 2)
            on(gate_matmul, s - 1)
            on(turn_inputs, s + 1)
            on(copy_inputs_out, s)
            on(difference, s)
            on(blend, s - 2)
            on(blend_mean, s - 3)
            on(blend_variance, s - 3)
            on(quantise_inputs, s)
            on(gate_sigmoid, s - 1)

            if r == 1:
                prepare_second_half()
            on(blend_deviation, r + 1)
            on(output_mean, r - 3)
            on(output_scale, r - 4)
            on(normalise, r)
            on(quantise_state, r - 2)
            on(output_matmul, r - 2)
            on(apply_gain, r - 1)
            on(output_shift, r - 4)
            on(blend_scale, r + 1)
            on(turn_normed, r)
            on(group_state, r - 1)
            on(store_state, r - 4)
            on(add_bias, r - 2)
            on(turn_state_back, r - 3)
            on(output_variance, r - 3)
            on(output_gain, r - 3)
            on(output_deviation, r - 3)
